import numpy as np
import ml_dtypes


def mxq(x, axis, fmt="e4m3"):
    dtype, down = {"e4m3": (ml_dtypes.float8_e4m3fn, 7), "e5m2": (ml_dtypes.float8_e5m2, 14)}[fmt]
    v = np.moveaxis(np.asarray(x, np.float32).astype(ml_dtypes.bfloat16).astype(np.float64), axis, -1)
    blocks = v.reshape(v.shape[:-1] + (-1, 32))
    amax = np.abs(blocks).max(-1, keepdims=True)
    byte = np.maximum(np.where(amax > 0, np.frexp(amax)[1] - 1 + 127, 0) - down, 1)
    scale = np.exp2(byte - 127.0)
    codes = (blocks / scale).astype(np.float32).astype(dtype).astype(np.float64)
    return np.moveaxis((codes * scale).reshape(v.shape), -1, axis)


WIDE = False


def mx_kscale(k):
    if not WIDE:
        return np.ones(k)
    levels = np.array([10, -10, 5, -5, 0])
    a = np.random.permutation(np.resize(levels, k // 512 * 4)).reshape(k // 512, 4)
    idx = np.arange(k)
    return np.exp2(a[idx // 512, idx % 128 // 32])


BF16 = ml_dtypes.bfloat16


def bf(x):
    return np.asarray(x, np.float32).astype(BF16)


def f64(x):
    return np.asarray(x).astype(np.float64)


B, I, H = 1024, 512, 512


def sig(v):
    return 1.0 / (1.0 + np.exp(-v))


def setup_inputs():
    s, t = mx_kscale(I), mx_kscale(H)
    return {"x": bf(np.random.standard_normal((B, I)) * s),
            "m_prev": bf(np.random.standard_normal((B, H)) * t),
            "c_prev": bf(np.random.standard_normal((B, H))),
            "w_m": bf(np.random.standard_normal((H, 8 * H)) / np.sqrt(H) / t[:, None]),
            "w_inputs": bf(np.random.standard_normal((I, 8 * H)) / np.sqrt(I) / s[:, None])}


def reference(x, m_prev, c_prev, w_m, w_inputs):
    m_mat = mxq(f64(m_prev), 1, "e4m3") @ mxq(f64(w_m), 0, "e4m3")
    in_mat = mxq(f64(x), 1, "e4m3") @ mxq(f64(w_inputs), 0, "e4m3")
    ms = np.split(m_mat, 8, axis=1)
    xs = np.split(in_mat, 8, axis=1)
    l1_0 = sig(xs[0] + ms[0])
    l1_1 = np.maximum(xs[1] + ms[1], 0.0)
    l1_2 = sig(xs[2] + ms[2])
    l1_3 = np.maximum(xs[3] * ms[3], 0.0)
    l1_4 = np.tanh(xs[4] + ms[4])
    l1_5 = sig(xs[5] + ms[5])
    l1_6 = np.tanh(xs[6] + ms[6])
    l1_7 = sig(xs[7] + ms[7])
    l2_0 = np.tanh(l1_0 * l1_1)
    l2_1 = np.tanh(l1_2 + l1_3)
    l2_2 = np.tanh(l1_4 * l1_5)
    l2_3 = sig(l1_6 + l1_7)
    l2_0 = np.tanh(l2_0 + f64(c_prev))
    new_c = l2_0 * l2_1
    l3_1 = np.tanh(l2_2 + l2_3)
    new_m = np.tanh(new_c * l3_1)
    return (new_m, new_c)

@@ -1,0 +1,225 @@
+from contextlib import ExitStack
+
+import concourse.mybir as mybir
+from concourse.masks import make_identity
+
+F32 = mybir.dt.float32
+BF16 = mybir.dt.bfloat16
+U32 = mybir.dt.uint32
+U8 = mybir.dt.uint8
+FP8X4 = mybir.dt.float8_e4m3fn_x4
+TANH = mybir.ActivationFunctionType.Tanh
+ADD = mybir.AluOpType.add
+MULT = mybir.AluOpType.mult
+MAX = mybir.AluOpType.max
+
+P = 128
+PACK = 4
+B = 1024
+K = 512
+H = 512
+T = B // P
+FLOPS = 2 * 2 * B * K * 8 * H
+
+CHUNKS = [("x", 3), ("x", 4), ("m", 4), ("x", 5), ("m", 5), ("x", 6), ("m", 6), ("x", 7), ("m", 7),
+          ("x", 2), ("m", 2), ("m", 3), ("x", 0), ("m", 0), ("x", 1), ("m", 1)]
+RAW_BUFS = 8
+
+
+def tile_nascell_kernel(tc, x, m_prev, c_prev, w_m, w_inputs, out_0, out_1):
+    nc = tc.nc
+    with ExitStack() as ctx:
+        keep = ctx.enter_context(tc.tile_pool(name="keep", bufs=1))
+        rawp = ctx.enter_context(tc.tile_pool(name="rawp", bufs=RAW_BUFS))
+        grpp = ctx.enter_context(tc.tile_pool(name="grpp", bufs=4))
+        psum = ctx.enter_context(tc.psum_pool(name="psum", bufs=8))
+        ctx.enter_context(tc.manual_schedule())
+
+        ident = keep.tile([P, P], F32)
+        make_identity(nc, ident[:])
+        half = keep.tile([P, 1], F32)
+        nc.vector.memset(half[:], 0.5)
+        quarter = keep.tile([P, 1], F32)
+        nc.vector.memset(quarter[:], 0.25)
+
+        act_dram = {"x": x.rearrange("(p t) k -> p t k", t=T), "m": m_prev.rearrange("(p t) k -> p t k", t=T)}
+        w_dram = {"x": w_inputs, "m": w_m}
+        a_raw = {}
+        a_grp = {}
+        a_codes = {}
+        a_scales = {}
+        for a in ("x", "m"):
+            a_raw[a] = keep.tile([P, T, K], BF16, name="a_raw_%s" % a)
+            a_grp[a] = keep.tile([P, T, P, PACK], BF16, name="a_grp_%s" % a, align_bytes=64)
+            a_codes[a] = keep.tile([P, T * P], U32, name="a_codes_%s" % a, align_bytes=64)
+            a_scales[a] = keep.tile([P, T * P], U8, name="a_scales_%s" % a, align_bytes=64)
+        w_codes = {}
+        w_scales = {}
+        for a, g in CHUNKS:
+            w_codes[(a, g)] = keep.tile([P, H], U32, name="w_codes_%s%d" % (a, g), align_bytes=64)
+            w_scales[(a, g)] = keep.tile([P, H], U8, name="w_scales_%s%d" % (a, g), align_bytes=64)
+        c_sb = keep.tile([P, T, H], BF16)
+        z1 = keep.tile([P, T, H], F32)
+        z2 = keep.tile([P, T, H], F32)
+        z3 = keep.tile([P, T, H], F32)
+        z4 = keep.tile([P, T, H], F32)
+        z5 = keep.tile([P, T, H], F32)
+        new_m_dram = out_0.rearrange("(p t) h -> p t h", t=T)
+        new_c_dram = out_1.rearrange("(p t) h -> p t h", t=T)
+
+        raw_tiles = {}
+        grp_tiles = {}
+
+        def load_chunk(n):
+            a, g = CHUNKS[n]
+            raw = rawp.tile([P, PACK, H], BF16)
+            nc.sync.dma_start(out=raw[:], in_=w_dram[a][:, g * H:(g + 1) * H].rearrange("(p j) c -> p j c", j=PACK))
+            raw_tiles[n] = raw
+
+        def load_act(a):
+            for j in range(T // 2):
+                nc.sync.dma_start(out=a_raw[a][:, 2 * j:2 * j + 2, :], in_=act_dram[a][:, 2 * j:2 * j + 2, :])
+
+        def regroup(n):
+            grouped = grpp.tile([P, H, PACK], BF16, align_bytes=64)
+            nc.vector.tensor_copy(
+                out=grouped[:].rearrange("p (c i) t -> p c t i", i=4),
+                in_=raw_tiles[n][:].rearrange("p t (c i) -> p c t i", i=4),
+            )
+            grp_tiles[n] = grouped
+            if n + RAW_BUFS < len(CHUNKS):
+                load_chunk(n + RAW_BUFS)
+            if n + RAW_BUFS == len(CHUNKS) - 1:
+                nc.sync.dma_start(out=c_sb[:], in_=c_prev.rearrange("(p t) h -> p t h", t=T))
+
+        def quantise(n):
+            nc.vector.quantize_mx(
+                out=w_codes[CHUNKS[n]][:].bitcast(FP8X4),
+                scales=w_scales[CHUNKS[n]][:],
+                in_=grp_tiles[n][:].rearrange("p c t -> p (c t)"),
+            )
+
+        def prepare(first, count):
+            for n in range(first, first + count):
+                regroup(n)
+            for n in range(first, first + count):
+                quantise(n)
+
+        def transpose_act(a):
+            words = a_raw[a][:].bitcast(F32).rearrange("p t (q u) -> p t u q", u=2)
+            banks = []
+            for j in range(T // 2):
+                acc = psum.tile([P, 2, 2, P], F32)
+                for tt in range(2):
+                    for u in range(2):
+                        nc.tensor.transpose(acc[:, tt, u, :], words[:, 2 * j + tt, u, :], ident[:])
+                banks.append(acc)
+            return banks
+
+        def copy_act(a, banks):
+            grp_words = a_grp[a][:].bitcast(F32)
+            for j in range(T // 2):
+                nc.scalar.copy(out=grp_words[:, 2 * j:2 * j + 2, :, :], in_=banks[j][:].rearrange("p t u b -> p t b u"))
+
+        def quantise_act(a):
+            for j in range(T // 2):
+                cols = slice(2 * j * P, (2 * j + 2) * P)
+                nc.vector.quantize_mx(
+                    out=a_codes[a][:, cols].bitcast(FP8X4),
+                    scales=a_scales[a][:, cols],
+                    in_=a_grp[a][:, 2 * j:2 * j + 2, :, :].rearrange("p t b j -> p (t b j)"),
+                )
+
+        def matmuls(g, sides):
+            banks = []
+            for i in range(T):
+                acc = psum.tile([P, H], F32)
+                rows = slice(i * P, (i + 1) * P)
+                for s, a in enumerate(sides):
+                    nc.tensor.matmul_mx(
+                        out=acc[:],
+                        lhsT=a_codes[a][:, rows].bitcast(FP8X4),
+                        lhsT_scale=a_scales[a][:, rows],
+                        rhs=w_codes[(a, g)][:].bitcast(FP8X4),
+                        rhs_scale=w_scales[(a, g)][:],
+                        start=(s == 0),
+                        stop=(s == len(sides) - 1),
+                    )
+                banks.append(acc)
+            return banks
+
+        def tanh_pass(dst, src, scale, bias=None):
+            for i in range(T):
+                in_ = src[i][:] if isinstance(src, list) else src[:, i, :]
+                if bias is None:
+                    nc.scalar.activation(out=dst[:, i, :], in_=in_, func=TANH, scale=scale)
+                else:
+                    nc.scalar.activation(out=dst[:, i, :], in_=in_, func=TANH, scale=scale, bias=bias[:])
+
+        def stt_pass(dst, in0, scalar, op0, in1, op1):
+            for i in range(T):
+                a0 = in0[i][:] if isinstance(in0, list) else in0[:, i, :]
+                a1 = in1[i][:] if isinstance(in1, list) else in1[:, i, :]
+                nc.vector.scalar_tensor_tensor(out=dst[:, i, :], in0=a0, scalar=scalar, in1=a1, op0=op0, op1=op1)
+
+        load_chunk(0)
+        load_act("x")
+        load_chunk(1)
+        load_chunk(2)
+        load_act("m")
+        for n in range(3, RAW_BUFS):
+            load_chunk(n)
+
+        tx = transpose_act("x")
+        copy_act("x", tx)
+        prepare(0, 1)
+        quantise_act("x")
+        x3 = matmuls(3, ("x",))
+        for i in range(T):
+            nc.scalar.copy(out=z1[:, i, :], in_=x3[i][:])
+        tm = transpose_act("m")
+        copy_act("m", tm)
+        prepare(1, 2)
+        quantise_act("m")
+        g4 = matmuls(4, ("x", "m"))
+        tanh_pass(z2, g4, 1.0)
+        prepare(3, 2)
+        g5 = matmuls(5, ("x", "m"))
+        tanh_pass(z3, g5, 0.5)
+        prepare(5, 2)
+        g6 = matmuls(6, ("x", "m"))
+        tanh_pass(z4, g6, 1.0)
+        prepare(7, 2)
+        g7 = matmuls(7, ("x", "m"))
+        tanh_pass(z5, g7, 0.5)
+        stt_pass(z2, z3, 1.0, ADD, z2, MULT)
+        tanh_pass(z2, z2, 0.5)
+        prepare(9, 2)
+        prepare(11, 1)
+        m3 = matmuls(3, ("m",))
+        stt_pass(z1, m3, 2.0, MULT, z1, MULT)
+        g2 = matmuls(2, ("x", "m"))
+        tanh_pass(z3, g2, 0.5)
+        stt_pass(z4, z5, 0.5, MULT, z4, ADD)
+        tanh_pass(z4, z4, 0.5, quarter)
+        prepare(12, 2)
+        g0 = matmuls(0, ("x", "m"))
+        tanh_pass(z5, g0, 0.5)
+        prepare(14, 2)
+        g1 = matmuls(1, ("x", "m"))
+        stt_pass(z1, z1, 0.0, MAX, z3, ADD)
+        tanh_pass(z1, z1, 0.5, half)
+        stt_pass(z5, z5, 1.0, ADD, g1, MULT)
+        tanh_pass(z5, z5, 0.5)
+        stt_pass(z2, z4, 0.5, MULT, z2, ADD)
+        stt_pass(z5, z5, 0.0, MAX, c_sb, ADD)
+        tanh_pass(z5, z5, 1.0)
+        for i in range(T):
+            nc.vector.tensor_tensor(out=z5[:, i, :], in0=z5[:, i, :], in1=z1[:, i, :], op=MULT)
+            nc.sync.dma_start(out=new_c_dram[:, i, :], in_=z5[:, i, :])
+        tanh_pass(z2, z2, 1.0, half)
+        for i in range(T):
+            nc.vector.tensor_tensor(out=z2[:, i, :], in0=z2[:, i, :], in1=z5[:, i, :], op=MULT)
+        for i in range(T):
+            nc.scalar.activation(out=z2[:, i, :], in_=z2[:, i, :], func=TANH)
+            nc.sync.dma_start(out=new_m_dram[:, i, :], in_=z2[:, i, :])

@@ -9,6 +9,7 @@ U32 = mybir.dt.uint32
 U8 = mybir.dt.uint8
 FP8X4 = mybir.dt.float8_e4m3fn_x4
 TANH = mybir.ActivationFunctionType.Tanh
+SIGMOID = mybir.ActivationFunctionType.Sigmoid
 ADD = mybir.AluOpType.add
 MULT = mybir.AluOpType.mult
 MAX = mybir.AluOpType.max
@@ -31,16 +32,15 @@ def tile_nascell_kernel(tc, x, m_prev, c_prev, w_m, w_inputs, out_0, out_1):
     with ExitStack() as ctx:
         keep = ctx.enter_context(tc.tile_pool(name="keep", bufs=1))
         rawp = ctx.enter_context(tc.tile_pool(name="rawp", bufs=RAW_BUFS))
-        grpp = ctx.enter_context(tc.tile_pool(name="grpp", bufs=4))
+        grpp = ctx.enter_context(tc.tile_pool(name="grpp", bufs=5))
         psum = ctx.enter_context(tc.psum_pool(name="psum", bufs=8))
         ctx.enter_context(tc.manual_schedule())
 
+        warm = keep.tile([P, 1], F32)
+        nc.vector.memset(warm[:], 0.0)
+        nc.scalar.activation(out=warm[:], in_=warm[:], func=SIGMOID)
         ident = keep.tile([P, P], F32)
         make_identity(nc, ident[:])
-        half = keep.tile([P, 1], F32)
-        nc.vector.memset(half[:], 0.5)
-        quarter = keep.tile([P, 1], F32)
-        nc.vector.memset(quarter[:], 0.25)
 
         act_dram = {"x": x.rearrange("(p t) k -> p t k", t=T), "m": m_prev.rearrange("(p t) k -> p t k", t=T)}
         w_dram = {"x": w_inputs, "m": w_m}
@@ -80,12 +80,14 @@ def tile_nascell_kernel(tc, x, m_prev, c_prev, w_m, w_inputs, out_0, out_1):
             for j in range(T // 2):
                 nc.sync.dma_start(out=a_raw[a][:, 2 * j:2 * j + 2, :], in_=act_dram[a][:, 2 * j:2 * j + 2, :])
 
-        def regroup(n):
+        def regroup(n, on_scalar=False):
             grouped = grpp.tile([P, H, PACK], BF16, align_bytes=64)
-            nc.vector.tensor_copy(
-                out=grouped[:].rearrange("p (c i) t -> p c t i", i=4),
-                in_=raw_tiles[n][:].rearrange("p t (c i) -> p c t i", i=4),
-            )
+            dst = grouped[:].rearrange("p (c i) t -> p c t i", i=4)
+            src = raw_tiles[n][:].rearrange("p t (c i) -> p c t i", i=4)
+            if on_scalar:
+                nc.scalar.copy(out=dst, in_=src)
+            else:
+                nc.vector.tensor_copy(out=dst, in_=src)
             grp_tiles[n] = grouped
             if n + RAW_BUFS < len(CHUNKS):
                 load_chunk(n + RAW_BUFS)
@@ -148,19 +150,20 @@ def tile_nascell_kernel(tc, x, m_prev, c_prev, w_m, w_inputs, out_0, out_1):
                 banks.append(acc)
             return banks
 
-        def tanh_pass(dst, src, scale, bias=None):
+        def act_pass(func, dst, src):
             for i in range(T):
                 in_ = src[i][:] if isinstance(src, list) else src[:, i, :]
-                if bias is None:
-                    nc.scalar.activation(out=dst[:, i, :], in_=in_, func=TANH, scale=scale)
-                else:
-                    nc.scalar.activation(out=dst[:, i, :], in_=in_, func=TANH, scale=scale, bias=bias[:])
+                nc.scalar.activation(out=dst[:, i, :], in_=in_, func=func)
 
-        def stt_pass(dst, in0, scalar, op0, in1, op1):
-            for i in range(T):
+        def tt_pass(dst, in0, in1, op, tiles=range(T), eng=None):
+            for i in tiles:
                 a0 = in0[i][:] if isinstance(in0, list) else in0[:, i, :]
                 a1 = in1[i][:] if isinstance(in1, list) else in1[:, i, :]
-                nc.vector.scalar_tensor_tensor(out=dst[:, i, :], in0=a0, scalar=scalar, in1=a1, op0=op0, op1=op1)
+                (eng or nc.vector).tensor_tensor(out=dst[:, i, :], in0=a0, in1=a1, op=op)
+
+        def relu_add_pass(dst, in0, in1):
+            for i in range(T):
+                nc.vector.scalar_tensor_tensor(out=dst[:, i, :], in0=in0[:, i, :], scalar=0.0, in1=in1[:, i, :], op0=MAX, op1=ADD)
 
         load_chunk(0)
         load_act("x")
@@ -180,46 +183,55 @@ def tile_nascell_kernel(tc, x, m_prev, c_prev, w_m, w_inputs, out_0, out_1):
         tm = transpose_act("m")
         copy_act("m", tm)
         prepare(1, 2)
+        regroup(3)
+        regroup(4)
         quantise_act("m")
         g4 = matmuls(4, ("x", "m"))
-        tanh_pass(z2, g4, 1.0)
-        prepare(3, 2)
+        act_pass(TANH, z2, g4)
+        quantise(3)
+        quantise(4)
         g5 = matmuls(5, ("x", "m"))
-        tanh_pass(z3, g5, 0.5)
+        act_pass(SIGMOID, z3, g5)
         prepare(5, 2)
         g6 = matmuls(6, ("x", "m"))
-        tanh_pass(z4, g6, 1.0)
+        act_pass(TANH, z4, g6)
         prepare(7, 2)
         g7 = matmuls(7, ("x", "m"))
-        tanh_pass(z5, g7, 0.5)
-        stt_pass(z2, z3, 1.0, ADD, z2, MULT)
-        tanh_pass(z2, z2, 0.5)
-        prepare(9, 2)
-        prepare(11, 1)
+        act_pass(SIGMOID, z5, g7)
+        tt_pass(z2, z2, z3, MULT)
+        act_pass(TANH, z2, z2)
+        regroup(9)
+        regroup(10)
+        regroup(11)
+        quantise(11)
+        quantise(9)
+        quantise(10)
         m3 = matmuls(3, ("m",))
-        stt_pass(z1, m3, 2.0, MULT, z1, MULT)
+        tt_pass(z1, z1, m3, MULT)
         g2 = matmuls(2, ("x", "m"))
-        tanh_pass(z3, g2, 0.5)
-        stt_pass(z4, z5, 0.5, MULT, z4, ADD)
-        tanh_pass(z4, z4, 0.5, quarter)
+        act_pass(SIGMOID, z3, g2)
+        regroup(15, on_scalar=True)
+        tt_pass(z4, z4, z5, ADD)
+        act_pass(SIGMOID, z4, z4)
         prepare(12, 2)
         g0 = matmuls(0, ("x", "m"))
-        tanh_pass(z5, g0, 0.5)
-        prepare(14, 2)
+        act_pass(SIGMOID, z5, g0)
+        regroup(14)
+        quantise(14)
+        quantise(15)
         g1 = matmuls(1, ("x", "m"))
-        stt_pass(z1, z1, 0.0, MAX, z3, ADD)
-        tanh_pass(z1, z1, 0.5, half)
-        stt_pass(z5, z5, 1.0, ADD, g1, MULT)
-        tanh_pass(z5, z5, 0.5)
-        stt_pass(z2, z4, 0.5, MULT, z2, ADD)
-        stt_pass(z5, z5, 0.0, MAX, c_sb, ADD)
-        tanh_pass(z5, z5, 1.0)
+        relu_add_pass(z1, z1, z3)
+        act_pass(TANH, z1, z1)
+        tt_pass(z5, z5, g1, MULT)
+        act_pass(TANH, z5, z5)
+        tt_pass(z2, z2, z4, ADD)
+        relu_add_pass(z5, z5, c_sb)
+        act_pass(TANH, z5, z5)
         for i in range(T):
             nc.vector.tensor_tensor(out=z5[:, i, :], in0=z5[:, i, :], in1=z1[:, i, :], op=MULT)
             nc.sync.dma_start(out=new_c_dram[:, i, :], in_=z5[:, i, :])
-        tanh_pass(z2, z2, 1.0, half)
-        for i in range(T):
-            nc.vector.tensor_tensor(out=z2[:, i, :], in0=z2[:, i, :], in1=z5[:, i, :], op=MULT)
+        act_pass(TANH, z2, z2)
+        tt_pass(z2, z2, z5, MULT)
         for i in range(T):
             nc.scalar.activation(out=z2[:, i, :], in_=z2[:, i, :], func=TANH)
             nc.sync.dma_start(out=new_m_dram[:, i, :], in_=z2[:, i, :])

@@ -207,24 +207,26 @@ def tile_nascell_kernel(tc, x, m_prev, c_prev, w_m, w_inputs, out_0, out_1):
         quantise(9)
         quantise(10)
         m3 = matmuls(3, ("m",))
+        tt_pass(z4, z4, z5, ADD, range(0, 4), nc.gpsimd)
         tt_pass(z1, z1, m3, MULT)
         g2 = matmuls(2, ("x", "m"))
         act_pass(SIGMOID, z3, g2)
-        regroup(15, on_scalar=True)
-        tt_pass(z4, z4, z5, ADD)
+        tt_pass(z4, z4, z5, ADD, range(4, T))
         act_pass(SIGMOID, z4, z4)
         prepare(12, 2)
         g0 = matmuls(0, ("x", "m"))
         act_pass(SIGMOID, z5, g0)
         regroup(14)
+        regroup(15)
         quantise(14)
         quantise(15)
         g1 = matmuls(1, ("x", "m"))
         relu_add_pass(z1, z1, z3)
         act_pass(TANH, z1, z1)
+        tt_pass(z2, z2, z4, ADD, range(0, 4), nc.gpsimd)
         tt_pass(z5, z5, g1, MULT)
         act_pass(TANH, z5, z5)
-        tt_pass(z2, z2, z4, ADD)
+        tt_pass(z2, z2, z4, ADD, range(4, T))
         relu_add_pass(z5, z5, c_sb)
         act_pass(TANH, z5, z5)
         for i in range(T):

@@ -25,6 +25,9 @@ FLOPS = 2 * 2 * B * K * 8 * H
 CHUNKS = [("x", 3), ("x", 4), ("m", 4), ("x", 5), ("m", 5), ("x", 6), ("m", 6), ("x", 7), ("m", 7),
           ("x", 2), ("m", 2), ("m", 3), ("x", 0), ("m", 0), ("x", 1), ("m", 1)]
 RAW_BUFS = 8
+SINGLE = [(i, i + 1) for i in range(T)]
+PAIRS = [(i, i + 2) for i in range(0, T, 2)]
+WIDE = PAIRS
 
 
 def tile_nascell_kernel(tc, x, m_prev, c_prev, w_m, w_inputs, out_0, out_1):
@@ -76,18 +79,16 @@ def tile_nascell_kernel(tc, x, m_prev, c_prev, w_m, w_inputs, out_0, out_1):
             nc.sync.dma_start(out=raw[:], in_=w_dram[a][:, g * H:(g + 1) * H].rearrange("(p j) c -> p j c", j=PACK))
             raw_tiles[n] = raw
 
-        def load_act(a):
-            for j in range(T // 2):
+        def load_act(a, pieces):
+            for j in pieces:
                 nc.sync.dma_start(out=a_raw[a][:, 2 * j:2 * j + 2, :], in_=act_dram[a][:, 2 * j:2 * j + 2, :])
 
-        def regroup(n, on_scalar=False):
+        def regroup(n):
             grouped = grpp.tile([P, H, PACK], BF16, align_bytes=64)
-            dst = grouped[:].rearrange("p (c i) t -> p c t i", i=4)
-            src = raw_tiles[n][:].rearrange("p t (c i) -> p c t i", i=4)
-            if on_scalar:
-                nc.scalar.copy(out=dst, in_=src)
-            else:
-                nc.vector.tensor_copy(out=dst, in_=src)
+            nc.vector.tensor_copy(
+                out=grouped[:].rearrange("p (c i) t -> p c t i", i=4),
+                in_=raw_tiles[n][:].rearrange("p t (c i) -> p c t i", i=4),
+            )
             grp_tiles[n] = grouped
             if n + RAW_BUFS < len(CHUNKS):
                 load_chunk(n + RAW_BUFS)
@@ -107,10 +108,10 @@ def tile_nascell_kernel(tc, x, m_prev, c_prev, w_m, w_inputs, out_0, out_1):
             for n in range(first, first + count):
                 quantise(n)
 
-        def transpose_act(a):
+        def transpose_act(a, pieces):
             words = a_raw[a][:].bitcast(F32).rearrange("p t (q u) -> p t u q", u=2)
             banks = []
-            for j in range(T // 2):
+            for j in pieces:
                 acc = psum.tile([P, 2, 2, P], F32)
                 for tt in range(2):
                     for u in range(2):
@@ -118,13 +119,13 @@ def tile_nascell_kernel(tc, x, m_prev, c_prev, w_m, w_inputs, out_0, out_1):
                 banks.append(acc)
             return banks
 
-        def copy_act(a, banks):
+        def copy_act(a, pieces, banks):
             grp_words = a_grp[a][:].bitcast(F32)
-            for j in range(T // 2):
-                nc.scalar.copy(out=grp_words[:, 2 * j:2 * j + 2, :, :], in_=banks[j][:].rearrange("p t u b -> p t b u"))
+            for j, bank in zip(pieces, banks):
+                nc.scalar.copy(out=grp_words[:, 2 * j:2 * j + 2, :, :], in_=bank[:].rearrange("p t u b -> p t b u"))
 
-        def quantise_act(a):
-            for j in range(T // 2):
+        def quantise_act(a, pieces):
+            for j in pieces:
                 cols = slice(2 * j * P, (2 * j + 2) * P)
                 nc.vector.quantize_mx(
                     out=a_codes[a][:, cols].bitcast(FP8X4),
@@ -150,56 +151,61 @@ def tile_nascell_kernel(tc, x, m_prev, c_prev, w_m, w_inputs, out_0, out_1):
                 banks.append(acc)
             return banks
 
-        def act_pass(func, dst, src):
-            for i in range(T):
-                in_ = src[i][:] if isinstance(src, list) else src[:, i, :]
-                nc.scalar.activation(out=dst[:, i, :], in_=in_, func=func)
+        def act_banks(func, dst, banks, first=0):
+            for i, bank in enumerate(banks):
+                nc.scalar.activation(out=dst[:, first + i, :], in_=bank[:], func=func)
 
-        def tt_pass(dst, in0, in1, op, tiles=range(T), eng=None):
-            for i in tiles:
-                a0 = in0[i][:] if isinstance(in0, list) else in0[:, i, :]
-                a1 = in1[i][:] if isinstance(in1, list) else in1[:, i, :]
-                (eng or nc.vector).tensor_tensor(out=dst[:, i, :], in0=a0, in1=a1, op=op)
+        def act_pass(func, z, spans=WIDE):
+            for lo, hi in spans:
+                nc.scalar.activation(out=z[:, lo:hi, :], in_=z[:, lo:hi, :], func=func)
 
-        def relu_add_pass(dst, in0, in1):
-            for i in range(T):
-                nc.vector.scalar_tensor_tensor(out=dst[:, i, :], in0=in0[:, i, :], scalar=0.0, in1=in1[:, i, :], op0=MAX, op1=ADD)
+        def tt_banks(z, banks):
+            for i, bank in enumerate(banks):
+                nc.vector.tensor_tensor(out=z[:, i, :], in0=z[:, i, :], in1=bank[:], op=MULT)
+
+        def tt_pass(eng, z, other, op, spans):
+            for lo, hi in spans:
+                eng.tensor_tensor(out=z[:, lo:hi, :], in0=z[:, lo:hi, :], in1=other[:, lo:hi, :], op=op)
+
+        def relu_add_pass(z, other, spans=WIDE):
+            for lo, hi in spans:
+                nc.vector.scalar_tensor_tensor(out=z[:, lo:hi, :], in0=z[:, lo:hi, :], scalar=0.0, in1=other[:, lo:hi, :], op0=MAX, op1=ADD)
 
         load_chunk(0)
-        load_act("x")
+        load_act("x", (0, 1, 2, 3))
+        load_act("m", (0, 1))
         load_chunk(1)
         load_chunk(2)
-        load_act("m")
+        load_act("m", (2, 3))
         for n in range(3, RAW_BUFS):
             load_chunk(n)
 
-        tx = transpose_act("x")
-        copy_act("x", tx)
+        tx = transpose_act("x", (0, 1, 2, 3))
+        tm = transpose_act("m", (0, 1))
+        copy_act("x", (0, 1, 2, 3), tx)
+        copy_act("m", (0, 1), tm)
         prepare(0, 1)
-        quantise_act("x")
+        quantise_act("x", (0, 1, 2, 3))
+        quantise_act("m", (0, 1))
         x3 = matmuls(3, ("x",))
         for i in range(T):
             nc.scalar.copy(out=z1[:, i, :], in_=x3[i][:])
-        tm = transpose_act("m")
-        copy_act("m", tm)
-        prepare(1, 2)
-        regroup(3)
-        regroup(4)
-        quantise_act("m")
-        g4 = matmuls(4, ("x", "m"))
-        act_pass(TANH, z2, g4)
-        quantise(3)
-        quantise(4)
-        g5 = matmuls(5, ("x", "m"))
-        act_pass(SIGMOID, z3, g5)
+        tm = transpose_act("m", (2, 3))
+        copy_act("m", (2, 3), tm)
+        regroup(1)
+        quantise(1)
+        regroup(2)
+        quantise(2)
+        quantise_act("m", (2, 3))
+        act_banks(TANH, z2, matmuls(4, ("x", "m")))
+        prepare(3, 2)
+        act_banks(SIGMOID, z3, matmuls(5, ("x", "m")))
         prepare(5, 2)
-        g6 = matmuls(6, ("x", "m"))
-        act_pass(TANH, z4, g6)
+        act_banks(TANH, z4, matmuls(6, ("x", "m")))
         prepare(7, 2)
-        g7 = matmuls(7, ("x", "m"))
-        act_pass(SIGMOID, z5, g7)
-        tt_pass(z2, z2, z3, MULT)
-        act_pass(TANH, z2, z2)
+        act_banks(SIGMOID, z5, matmuls(7, ("x", "m")))
+        tt_pass(nc.vector, z2, z3, MULT, WIDE)
+        act_pass(TANH, z2)
         regroup(9)
         regroup(10)
         regroup(11)
@@ -207,33 +213,35 @@ def tile_nascell_kernel(tc, x, m_prev, c_prev, w_m, w_inputs, out_0, out_1):
         quantise(9)
         quantise(10)
         m3 = matmuls(3, ("m",))
-        tt_pass(z4, z4, z5, ADD, range(0, 4), nc.gpsimd)
-        tt_pass(z1, z1, m3, MULT)
-        g2 = matmuls(2, ("x", "m"))
-        act_pass(SIGMOID, z3, g2)
-        tt_pass(z4, z4, z5, ADD, range(4, T))
-        act_pass(SIGMOID, z4, z4)
+        tt_pass(nc.gpsimd, z4, z5, ADD, SINGLE[:4])
+        tt_banks(z1, m3)
+        act_banks(SIGMOID, z3, matmuls(2, ("x", "m")))
+        tt_pass(nc.vector, z4, z5, ADD, WIDE[len(WIDE) // 2:])
+        act_pass(SIGMOID, z4)
         prepare(12, 2)
-        g0 = matmuls(0, ("x", "m"))
-        act_pass(SIGMOID, z5, g0)
-        regroup(14)
-        regroup(15)
-        quantise(14)
-        quantise(15)
+        act_banks(SIGMOID, z5, matmuls(0, ("x", "m")))
+        prepare(14, 2)
         g1 = matmuls(1, ("x", "m"))
-        relu_add_pass(z1, z1, z3)
-        act_pass(TANH, z1, z1)
-        tt_pass(z2, z2, z4, ADD, range(0, 4), nc.gpsimd)
-        tt_pass(z5, z5, g1, MULT)
-        act_pass(TANH, z5, z5)
-        tt_pass(z2, z2, z4, ADD, range(4, T))
-        relu_add_pass(z5, z5, c_sb)
-        act_pass(TANH, z5, z5)
-        for i in range(T):
-            nc.vector.tensor_tensor(out=z5[:, i, :], in0=z5[:, i, :], in1=z1[:, i, :], op=MULT)
-            nc.sync.dma_start(out=new_c_dram[:, i, :], in_=z5[:, i, :])
-        act_pass(TANH, z2, z2)
-        tt_pass(z2, z2, z5, MULT)
-        for i in range(T):
-            nc.scalar.activation(out=z2[:, i, :], in_=z2[:, i, :], func=TANH)
-            nc.sync.dma_start(out=new_m_dram[:, i, :], in_=z2[:, i, :])
+        relu_add_pass(z1, z3)
+        act_pass(TANH, z1)
+        tt_pass(nc.gpsimd, z2, z4, ADD, SINGLE[:4])
+        tt_banks(z5, g1)
+        act_pass(TANH, z5)
+        sums = []
+        for i in range(4, T):
+            acc = psum.tile([P, H], F32)
+            nc.tensor.matmul(out=acc[:], lhsT=ident[:], rhs=z2[:, i, :], start=True, stop=False)
+            nc.tensor.matmul(out=acc[:], lhsT=ident[:], rhs=z4[:, i, :], start=False, stop=True)
+            sums.append(acc)
+        relu_add_pass(z5, c_sb)
+        act_pass(TANH, z5)
+        for lo, hi in WIDE:
+            nc.vector.tensor_tensor(out=z5[:, lo:hi, :], in0=z5[:, lo:hi, :], in1=z1[:, lo:hi, :], op=MULT)
+            nc.sync.dma_start(out=new_c_dram[:, lo:hi, :], in_=z5[:, lo:hi, :])
+        act_pass(TANH, z2, WIDE[:len(WIDE) // 2])
+        act_banks(TANH, z2, sums, 4)
+        last = WIDE[:-1] + SINGLE[-2:]
+        tt_pass(nc.vector, z2, z5, MULT, last)
+        for lo, hi in last:
+            nc.scalar.activation(out=z2[:, lo:hi, :], in_=z2[:, lo:hi, :], func=TANH)
+            nc.sync.dma_start(out=new_m_dram[:, lo:hi, :], in_=z2[:, lo:hi, :])

@@ -25,6 +25,7 @@ FLOPS = 2 * 2 * B * K * 8 * H
 CHUNKS = [("x", 3), ("x", 4), ("m", 4), ("x", 5), ("m", 5), ("x", 6), ("m", 6), ("x", 7), ("m", 7),
           ("x", 2), ("m", 2), ("m", 3), ("x", 0), ("m", 0), ("x", 1), ("m", 1)]
 RAW_BUFS = 8
+PAD = 48
 SINGLE = [(i, i + 1) for i in range(T)]
 PAIRS = [(i, i + 2) for i in range(0, T, 2)]
 WIDE = PAIRS
@@ -54,13 +55,13 @@ def tile_nascell_kernel(tc, x, m_prev, c_prev, w_m, w_inputs, out_0, out_1):
         for a in ("x", "m"):
             a_raw[a] = keep.tile([P, T, K], BF16, name="a_raw_%s" % a)
             a_grp[a] = keep.tile([P, T, P, PACK], BF16, name="a_grp_%s" % a, align_bytes=64)
-            a_codes[a] = keep.tile([P, T * P], U32, name="a_codes_%s" % a, align_bytes=64)
-            a_scales[a] = keep.tile([P, T * P], U8, name="a_scales_%s" % a, align_bytes=64)
+            a_codes[a] = keep.tile([P, PAD + T * P], U32, name="a_codes_%s" % a, align_bytes=256)
+            a_scales[a] = keep.tile([P, T, 2 * P], U8, name="a_scales_%s" % a, align_bytes=256)
         w_codes = {}
         w_scales = {}
         for a, g in CHUNKS:
-            w_codes[(a, g)] = keep.tile([P, H], U32, name="w_codes_%s%d" % (a, g), align_bytes=64)
-            w_scales[(a, g)] = keep.tile([P, H], U8, name="w_scales_%s%d" % (a, g), align_bytes=64)
+            w_codes[(a, g)] = keep.tile([P, H], U32, name="w_codes_%s%d" % (a, g), align_bytes=256)
+            w_scales[(a, g)] = keep.tile([P, H], U8, name="w_scales_%s%d" % (a, g), align_bytes=256)
         c_sb = keep.tile([P, T, H], BF16)
         z1 = keep.tile([P, T, H], F32)
         z2 = keep.tile([P, T, H], F32)
@@ -126,23 +127,23 @@ def tile_nascell_kernel(tc, x, m_prev, c_prev, w_m, w_inputs, out_0, out_1):
 
         def quantise_act(a, pieces):
             for j in pieces:
-                cols = slice(2 * j * P, (2 * j + 2) * P)
-                nc.vector.quantize_mx(
-                    out=a_codes[a][:, cols].bitcast(FP8X4),
-                    scales=a_scales[a][:, cols],
-                    in_=a_grp[a][:, 2 * j:2 * j + 2, :, :].rearrange("p t b j -> p (t b j)"),
-                )
+                for i in (2 * j, 2 * j + 1):
+                    nc.vector.quantize_mx(
+                        out=a_codes[a][:, PAD + i * P:PAD + (i + 1) * P].bitcast(FP8X4),
+                        scales=a_scales[a][:, i, 0:P],
+                        in_=a_grp[a][:, i, :, :].rearrange("p b j -> p (b j)"),
+                    )
 
         def matmuls(g, sides):
             banks = []
             for i in range(T):
                 acc = psum.tile([P, H], F32)
-                rows = slice(i * P, (i + 1) * P)
+                rows = slice(PAD + i * P, PAD + (i + 1) * P)
                 for s, a in enumerate(sides):
                     nc.tensor.matmul_mx(
                         out=acc[:],
                         lhsT=a_codes[a][:, rows].bitcast(FP8X4),
-                        lhsT_scale=a_scales[a][:, rows],
+                        lhsT_scale=a_scales[a][:, i, 0:P],
                         rhs=w_codes[(a, g)][:].bitcast(FP8X4),
                         rhs_scale=w_scales[(a, g)][:],
                         start=(s == 0),

@@ -217,8 +217,16 @@ def tile_nascell_kernel(tc, x, m_prev, c_prev, w_m, w_inputs, out_0, out_1):
         tt_pass(nc.gpsimd, z4, z5, ADD, SINGLE[:4])
         tt_banks(z1, m3)
         act_banks(SIGMOID, z3, matmuls(2, ("x", "m")))
-        tt_pass(nc.vector, z4, z5, ADD, WIDE[len(WIDE) // 2:])
-        act_pass(SIGMOID, z4)
+        flipped = []
+        for i in range(4, T):
+            acc = psum.tile([P, H], F32)
+            for s, z in enumerate((z4, z5)):
+                for q in range(4):
+                    nc.tensor.matmul(out=acc[:, q * P:(q + 1) * P], lhsT=z[:, i, q * P:(q + 1) * P], rhs=ident[:],
+                                     is_transpose=True, start=(s == 0 and q == 0), stop=(s == 1 and q == 3))
+            flipped.append(acc)
+        act_pass(SIGMOID, z4, WIDE[:len(WIDE) // 2])
+        act_banks(SIGMOID, z4, flipped, 4)
         prepare(12, 2)
         act_banks(SIGMOID, z5, matmuls(0, ("x", "m")))
         prepare(14, 2)
@@ -232,7 +240,9 @@ def tile_nascell_kernel(tc, x, m_prev, c_prev, w_m, w_inputs, out_0, out_1):
         for i in range(4, T):
             acc = psum.tile([P, H], F32)
             nc.tensor.matmul(out=acc[:], lhsT=ident[:], rhs=z2[:, i, :], start=True, stop=False)
-            nc.tensor.matmul(out=acc[:], lhsT=ident[:], rhs=z4[:, i, :], start=False, stop=True)
+            for q in range(4):
+                nc.tensor.matmul(out=acc[:, q * P:(q + 1) * P], lhsT=z4[:, i, q * P:(q + 1) * P], rhs=ident[:],
+                                 is_transpose=True, start=False, stop=(q == 3))
             sums.append(acc)
         relu_add_pass(z5, c_sb)
         act_pass(TANH, z5)

@@ -20,15 +20,13 @@ B = 1024
 K = 512
 H = 512
 T = B // P
+Q = H // P
 FLOPS = 2 * 2 * B * K * 8 * H
 
-CHUNKS = [("x", 3), ("x", 4), ("m", 4), ("x", 5), ("m", 5), ("x", 6), ("m", 6), ("x", 7), ("m", 7),
-          ("x", 2), ("m", 2), ("m", 3), ("x", 0), ("m", 0), ("x", 1), ("m", 1)]
+CHUNKS = [(a, g) for g in (6, 7, 4, 5, 0, 1) for a in ("x", "m")] + [("x", 3), ("x", 2), ("m", 2), ("m", 3)]
 RAW_BUFS = 8
-PAD = 48
-SINGLE = [(i, i + 1) for i in range(T)]
 PAIRS = [(i, i + 2) for i in range(0, T, 2)]
-WIDE = PAIRS
+LAG = 2
 
 
 def tile_nascell_kernel(tc, x, m_prev, c_prev, w_m, w_inputs, out_0, out_1):
@@ -36,7 +34,8 @@ def tile_nascell_kernel(tc, x, m_prev, c_prev, w_m, w_inputs, out_0, out_1):
     with ExitStack() as ctx:
         keep = ctx.enter_context(tc.tile_pool(name="keep", bufs=1))
         rawp = ctx.enter_context(tc.tile_pool(name="rawp", bufs=RAW_BUFS))
-        grpp = ctx.enter_context(tc.tile_pool(name="grpp", bufs=5))
+        grpp = ctx.enter_context(tc.tile_pool(name="grpp", bufs=4))
+        big = ctx.enter_context(tc.tile_pool(name="big", bufs=6))
         psum = ctx.enter_context(tc.psum_pool(name="psum", bufs=8))
         ctx.enter_context(tc.manual_schedule())
 
@@ -45,29 +44,25 @@ def tile_nascell_kernel(tc, x, m_prev, c_prev, w_m, w_inputs, out_0, out_1):
         nc.scalar.activation(out=warm[:], in_=warm[:], func=SIGMOID)
         ident = keep.tile([P, P], F32)
         make_identity(nc, ident[:])
+        ident_bf = keep.tile([P, P], BF16)
+        make_identity(nc, ident_bf[:])
 
+        sides = ("x", "m")
         act_dram = {"x": x.rearrange("(p t) k -> p t k", t=T), "m": m_prev.rearrange("(p t) k -> p t k", t=T)}
         w_dram = {"x": w_inputs, "m": w_m}
-        a_raw = {}
-        a_grp = {}
+        a_raw = big.tile([P, 2, T, K], BF16, tag="big", name="a_raw", align_bytes=64)
+        a_grp = big.tile([P, 2, T, P, PACK], BF16, tag="big", name="a_grp", align_bytes=64)
         a_codes = {}
         a_scales = {}
-        for a in ("x", "m"):
-            a_raw[a] = keep.tile([P, T, K], BF16, name="a_raw_%s" % a)
-            a_grp[a] = keep.tile([P, T, P, PACK], BF16, name="a_grp_%s" % a, align_bytes=64)
-            a_codes[a] = keep.tile([P, PAD + T * P], U32, name="a_codes_%s" % a, align_bytes=256)
-            a_scales[a] = keep.tile([P, T, 2 * P], U8, name="a_scales_%s" % a, align_bytes=256)
+        for a in sides:
+            a_codes[a] = keep.tile([P, T * P], U32, name="a_codes_%s" % a, align_bytes=64)
+            a_scales[a] = keep.tile([P, T * P], U8, name="a_scales_%s" % a, align_bytes=64)
         w_codes = {}
         w_scales = {}
         for a, g in CHUNKS:
-            w_codes[(a, g)] = keep.tile([P, H], U32, name="w_codes_%s%d" % (a, g), align_bytes=256)
-            w_scales[(a, g)] = keep.tile([P, H], U8, name="w_scales_%s%d" % (a, g), align_bytes=256)
+            w_codes[(a, g)] = keep.tile([P, H], U32, name="w_codes_%s%d" % (a, g), align_bytes=64)
+            w_scales[(a, g)] = keep.tile([P, H], U8, name="w_scales_%s%d" % (a, g), align_bytes=64)
         c_sb = keep.tile([P, T, H], BF16)
-        z1 = keep.tile([P, T, H], F32)
-        z2 = keep.tile([P, T, H], F32)
-        z3 = keep.tile([P, T, H], F32)
-        z4 = keep.tile([P, T, H], F32)
-        z5 = keep.tile([P, T, H], F32)
         new_m_dram = out_0.rearrange("(p t) h -> p t h", t=T)
         new_c_dram = out_1.rearrange("(p t) h -> p t h", t=T)
 
@@ -80,12 +75,11 @@ def tile_nascell_kernel(tc, x, m_prev, c_prev, w_m, w_inputs, out_0, out_1):
             nc.sync.dma_start(out=raw[:], in_=w_dram[a][:, g * H:(g + 1) * H].rearrange("(p j) c -> p j c", j=PACK))
             raw_tiles[n] = raw
 
-        def load_act(a, pieces):
-            for j in pieces:
-                nc.sync.dma_start(out=a_raw[a][:, 2 * j:2 * j + 2, :], in_=act_dram[a][:, 2 * j:2 * j + 2, :])
+        def load_act(s, j):
+            nc.sync.dma_start(out=a_raw[:, s, 2 * j:2 * j + 2, :], in_=act_dram[sides[s]][:, 2 * j:2 * j + 2, :])
 
         def regroup(n):
-            grouped = grpp.tile([P, H, PACK], BF16, align_bytes=64)
+            grouped = grpp.tile([P, H, PACK], BF16, tag="grouped", name="grouped", align_bytes=64)
             nc.vector.tensor_copy(
                 out=grouped[:].rearrange("p (c i) t -> p c t i", i=4),
                 in_=raw_tiles[n][:].rearrange("p t (c i) -> p c t i", i=4),
@@ -93,7 +87,7 @@ def tile_nascell_kernel(tc, x, m_prev, c_prev, w_m, w_inputs, out_0, out_1):
             grp_tiles[n] = grouped
             if n + RAW_BUFS < len(CHUNKS):
                 load_chunk(n + RAW_BUFS)
-            if n + RAW_BUFS == len(CHUNKS) - 1:
+            if n + RAW_BUFS == len(CHUNKS) - 5:
                 nc.sync.dma_start(out=c_sb[:], in_=c_prev.rearrange("(p t) h -> p t h", t=T))
 
         def quantise(n):
@@ -109,150 +103,164 @@ def tile_nascell_kernel(tc, x, m_prev, c_prev, w_m, w_inputs, out_0, out_1):
             for n in range(first, first + count):
                 quantise(n)
 
-        def transpose_act(a, pieces):
-            words = a_raw[a][:].bitcast(F32).rearrange("p t (q u) -> p t u q", u=2)
-            banks = []
-            for j in pieces:
-                acc = psum.tile([P, 2, 2, P], F32)
-                for tt in range(2):
-                    for u in range(2):
-                        nc.tensor.transpose(acc[:, tt, u, :], words[:, 2 * j + tt, u, :], ident[:])
-                banks.append(acc)
-            return banks
+        def new_bank():
+            bank = psum.tile([P, H], F32, tag="bank", name="bank")
+            return bank
 
-        def copy_act(a, pieces, banks):
-            grp_words = a_grp[a][:].bitcast(F32)
-            for j, bank in zip(pieces, banks):
-                nc.scalar.copy(out=grp_words[:, 2 * j:2 * j + 2, :, :], in_=bank[:].rearrange("p t u b -> p t b u"))
+        def transpose_act(s, j):
+            words = a_raw[:, s].bitcast(F32).rearrange("p t (q u) -> p t u q", u=2)
+            bank = new_bank()
+            for tt in range(2):
+                for u in range(2):
+                    nc.tensor.transpose(bank[:, (2 * tt + u) * P:(2 * tt + u + 1) * P], words[:, 2 * j + tt, u, :], ident[:])
+            return bank
 
-        def quantise_act(a, pieces):
-            for j in pieces:
-                for i in (2 * j, 2 * j + 1):
-                    nc.vector.quantize_mx(
-                        out=a_codes[a][:, PAD + i * P:PAD + (i + 1) * P].bitcast(FP8X4),
-                        scales=a_scales[a][:, i, 0:P],
-                        in_=a_grp[a][:, i, :, :].rearrange("p b j -> p (b j)"),
-                    )
+        def copy_act(s, j, bank):
+            nc.scalar.copy(out=a_grp[:, s].bitcast(F32)[:, 2 * j:2 * j + 2, :, :],
+                           in_=bank[:].rearrange("p (t u b) -> p t b u", t=2, u=2))
 
-        def matmuls(g, sides):
-            banks = []
-            for i in range(T):
-                acc = psum.tile([P, H], F32)
-                rows = slice(PAD + i * P, PAD + (i + 1) * P)
-                for s, a in enumerate(sides):
-                    nc.tensor.matmul_mx(
-                        out=acc[:],
-                        lhsT=a_codes[a][:, rows].bitcast(FP8X4),
-                        lhsT_scale=a_scales[a][:, i, 0:P],
-                        rhs=w_codes[(a, g)][:].bitcast(FP8X4),
-                        rhs_scale=w_scales[(a, g)][:],
-                        start=(s == 0),
-                        stop=(s == len(sides) - 1),
-                    )
-                banks.append(acc)
-            return banks
+        def quantise_act(s, j):
+            cols = slice(2 * j * P, (2 * j + 2) * P)
+            nc.vector.quantize_mx(
+                out=a_codes[sides[s]][:, cols].bitcast(FP8X4),
+                scales=a_scales[sides[s]][:, cols],
+                in_=a_grp[:, s, 2 * j:2 * j + 2].rearrange("p t b k -> p (t b k)"),
+            )
 
-        def act_banks(func, dst, banks, first=0):
-            for i, bank in enumerate(banks):
-                nc.scalar.activation(out=dst[:, first + i, :], in_=bank[:], func=func)
+        def mx_rows(g, i, which):
+            bank = new_bank()
+            rows = slice(i * P, (i + 1) * P)
+            for s, a in enumerate(which):
+                nc.tensor.matmul_mx(
+                    out=bank[:],
+                    lhsT=a_codes[a][:, rows].bitcast(FP8X4), lhsT_scale=a_scales[a][:, rows],
+                    rhs=w_codes[(a, g)][:].bitcast(FP8X4), rhs_scale=w_scales[(a, g)][:],
+                    start=(s == 0), stop=(s == len(which) - 1),
+                )
+            return bank
 
-        def act_pass(func, z, spans=WIDE):
-            for lo, hi in spans:
-                nc.scalar.activation(out=z[:, lo:hi, :], in_=z[:, lo:hi, :], func=func)
+        def mx_cols(g, j):
+            bank = new_bank()
+            cols = slice((j % Q) * P, (j % Q + 1) * P)
+            half = slice((j // Q) * H, (j // Q + 1) * H)
+            for s, a in enumerate(sides):
+                nc.tensor.matmul_mx(
+                    out=bank[:],
+                    lhsT=w_codes[(a, g)][:, cols].bitcast(FP8X4), lhsT_scale=w_scales[(a, g)][:, cols],
+                    rhs=a_codes[a][:, half].bitcast(FP8X4), rhs_scale=a_scales[a][:, half],
+                    start=(s == 0), stop=(s == 1),
+                )
+            return bank
 
-        def tt_banks(z, banks):
-            for i, bank in enumerate(banks):
-                nc.vector.tensor_tensor(out=z[:, i, :], in0=z[:, i, :], in1=bank[:], op=MULT)
+        def block(z, q, i):
+            return z[:, Q * (i // Q) + q, (i % Q) * P:(i % Q + 1) * P]
 
-        def tt_pass(eng, z, other, op, spans):
-            for lo, hi in spans:
-                eng.tensor_tensor(out=z[:, lo:hi, :], in0=z[:, lo:hi, :], in1=other[:, lo:hi, :], op=op)
+        def flip_add(i, terms, plain=None):
+            bank = new_bank()
+            if plain is not None:
+                nc.tensor.matmul(out=bank[:], lhsT=ident_bf[:], rhs=plain, start=True, stop=False)
+            count = 0
+            for z in terms:
+                for q in range(Q):
+                    count += 1
+                    nc.tensor.matmul(out=bank[:, q * P:(q + 1) * P], lhsT=block(z, q, i), rhs=ident[:], is_transpose=True,
+                                     start=(plain is None and count == 1), stop=(count == Q * len(terms)))
+            return bank
 
-        def relu_add_pass(z, other, spans=WIDE):
-            for lo, hi in spans:
-                nc.vector.scalar_tensor_tensor(out=z[:, lo:hi, :], in0=z[:, lo:hi, :], scalar=0.0, in1=other[:, lo:hi, :], op0=MAX, op1=ADD)
+        def act(func, dst, src):
+            nc.scalar.activation(out=dst, in_=src, func=func)
+
+        def gate_cols(g, func, dst):
+            for j in range(T):
+                act(func, dst[:, j, :], mx_cols(g, j)[:])
+
+        def zt(name):
+            z = big.tile([P, T, H], F32, tag="big", name=name, align_bytes=64)
+            return z
 
         load_chunk(0)
-        load_act("x", (0, 1, 2, 3))
-        load_act("m", (0, 1))
         load_chunk(1)
-        load_chunk(2)
-        load_act("m", (2, 3))
-        for n in range(3, RAW_BUFS):
+        for j in range(4):
+            load_act(0, j)
+            load_act(1, j)
+        for n in range(2, RAW_BUFS):
             load_chunk(n)
 
-        tx = transpose_act("x", (0, 1, 2, 3))
-        tm = transpose_act("m", (0, 1))
-        copy_act("x", (0, 1, 2, 3), tx)
-        copy_act("m", (0, 1), tm)
-        prepare(0, 1)
-        quantise_act("x", (0, 1, 2, 3))
-        quantise_act("m", (0, 1))
-        x3 = matmuls(3, ("x",))
+        prepare(0, 2)
+        for j in range(4):
+            bx = transpose_act(0, j)
+            bm = transpose_act(1, j)
+            copy_act(0, j, bx)
+            copy_act(1, j, bm)
+            quantise_act(0, j)
+            quantise_act(1, j)
+        z6 = zt("z6")
+        z7 = zt("z7")
+        z4 = zt("z4")
+        z5 = zt("z5")
+        prepare(2, 2)
+        gate_cols(6, TANH, z6)
+        prepare(4, 2)
+        gate_cols(7, SIGMOID, z7)
+        prepare(6, 2)
+        gate_cols(4, TANH, z4)
+        prepare(8, 2)
+        gate_cols(5, SIGMOID, z5)
+        prepare(10, 3)
+        z0 = zt("z0")
+        gate_cols(0, SIGMOID, z0)
+        for lo, hi in PAIRS:
+            nc.vector.tensor_tensor(out=z4[:, lo:hi, :], in0=z4[:, lo:hi, :], in1=z5[:, lo:hi, :], op=MULT)
+        for n, (lo, hi) in enumerate(PAIRS):
+            back = PAIRS[len(PAIRS) - 1 - n]
+            nc.gpsimd.tensor_tensor(out=z5[:, back[0]:back[1], :], in0=z6[:, lo:hi, :], in1=z7[:, lo:hi, :], op=ADD)
+        for j in range(T):
+            nc.vector.scalar_tensor_tensor(out=z0[:, j, :], in0=mx_cols(1, j)[:], scalar=0.0, in1=z0[:, j, :], op0=MAX, op1=MULT)
+        for lo, hi in PAIRS:
+            act(TANH, z4[:, lo:hi, :], z4[:, lo:hi, :])
+        zx = zt("zx")
         for i in range(T):
-            nc.scalar.copy(out=z1[:, i, :], in_=x3[i][:])
-        tm = transpose_act("m", (2, 3))
-        copy_act("m", (2, 3), tm)
-        regroup(1)
-        quantise(1)
-        regroup(2)
-        quantise(2)
-        quantise_act("m", (2, 3))
-        act_banks(TANH, z2, matmuls(4, ("x", "m")))
-        prepare(3, 2)
-        act_banks(SIGMOID, z3, matmuls(5, ("x", "m")))
-        prepare(5, 2)
-        act_banks(TANH, z4, matmuls(6, ("x", "m")))
-        prepare(7, 2)
-        act_banks(SIGMOID, z5, matmuls(7, ("x", "m")))
-        tt_pass(nc.vector, z2, z3, MULT, WIDE)
-        act_pass(TANH, z2)
-        regroup(9)
-        regroup(10)
-        regroup(11)
-        quantise(11)
-        quantise(9)
-        quantise(10)
-        m3 = matmuls(3, ("m",))
-        tt_pass(nc.gpsimd, z4, z5, ADD, SINGLE[:4])
-        tt_banks(z1, m3)
-        act_banks(SIGMOID, z3, matmuls(2, ("x", "m")))
-        flipped = []
-        for i in range(4, T):
-            acc = psum.tile([P, H], F32)
-            for s, z in enumerate((z4, z5)):
-                for q in range(4):
-                    nc.tensor.matmul(out=acc[:, q * P:(q + 1) * P], lhsT=z[:, i, q * P:(q + 1) * P], rhs=ident[:],
-                                     is_transpose=True, start=(s == 0 and q == 0), stop=(s == 1 and q == 3))
-            flipped.append(acc)
-        act_pass(SIGMOID, z4, WIDE[:len(WIDE) // 2])
-        act_banks(SIGMOID, z4, flipped, 4)
-        prepare(12, 2)
-        act_banks(SIGMOID, z5, matmuls(0, ("x", "m")))
-        prepare(14, 2)
-        g1 = matmuls(1, ("x", "m"))
-        relu_add_pass(z1, z3)
-        act_pass(TANH, z1)
-        tt_pass(nc.gpsimd, z2, z4, ADD, SINGLE[:4])
-        tt_banks(z5, g1)
-        act_pass(TANH, z5)
+            nc.vector.tensor_copy(out=zx[:, i, :], in_=mx_rows(3, i, ("x",))[:])
         sums = []
-        for i in range(4, T):
-            acc = psum.tile([P, H], F32)
-            nc.tensor.matmul(out=acc[:], lhsT=ident[:], rhs=z2[:, i, :], start=True, stop=False)
-            for q in range(4):
-                nc.tensor.matmul(out=acc[:, q * P:(q + 1) * P], lhsT=z4[:, i, q * P:(q + 1) * P], rhs=ident[:],
-                                 is_transpose=True, start=False, stop=(q == 3))
-            sums.append(acc)
-        relu_add_pass(z5, c_sb)
-        act_pass(TANH, z5)
-        for lo, hi in WIDE:
-            nc.vector.tensor_tensor(out=z5[:, lo:hi, :], in0=z5[:, lo:hi, :], in1=z1[:, lo:hi, :], op=MULT)
-            nc.sync.dma_start(out=new_c_dram[:, lo:hi, :], in_=z5[:, lo:hi, :])
-        act_pass(TANH, z2, WIDE[:len(WIDE) // 2])
-        act_banks(TANH, z2, sums, 4)
-        last = WIDE[:-1] + SINGLE[-2:]
-        tt_pass(nc.vector, z2, z5, MULT, last)
-        for lo, hi in last:
-            nc.scalar.activation(out=z2[:, lo:hi, :], in_=z2[:, lo:hi, :], func=TANH)
-            nc.sync.dma_start(out=new_m_dram[:, lo:hi, :], in_=z2[:, lo:hi, :])
+        for half in range(2):
+            for lo, hi in PAIRS[2 * half:2 * half + 2]:
+                act(TANH, z0[:, lo:hi, :], z0[:, lo:hi, :])
+            for i in range(Q * half, Q * half + Q):
+                sums.append(flip_add(i, (z0,), c_sb[:, i, :]))
+        prepare(13, 2)
+        prepare(15, 1)
+        for i in range(T):
+            act(TANH, z7[:, i, :], sums[i][:])
+        for n, (lo, hi) in enumerate(PAIRS):
+            back = PAIRS[len(PAIRS) - 1 - n]
+            act(SIGMOID, z6[:, lo:hi, :], z5[:, back[0]:back[1], :])
+        g2 = [mx_rows(2, i, sides) for i in range(Q)]
+        for i in range(T):
+            nc.vector.tensor_tensor(out=zx[:, i, :], in0=zx[:, i, :], in1=mx_rows(3, i, ("m",))[:], op=MULT)
+        g2 += [mx_rows(2, i, sides) for i in range(Q, T)]
+        for i in range(T):
+            act(SIGMOID, z0[:, i, :], g2[i][:])
+        for lo, hi in PAIRS:
+            nc.vector.scalar_tensor_tensor(out=zx[:, lo:hi, :], in0=zx[:, lo:hi, :], scalar=0.0, in1=z0[:, lo:hi, :], op0=MAX, op1=ADD)
+        for lo, hi in PAIRS:
+            act(TANH, zx[:, lo:hi, :], zx[:, lo:hi, :])
+        def new_c(n):
+            lo, hi = PAIRS[n]
+            nc.vector.tensor_tensor(out=z7[:, lo:hi, :], in0=z7[:, lo:hi, :], in1=zx[:, lo:hi, :], op=MULT)
+            nc.sync.dma_start(out=new_c_dram[:, lo:hi, :], in_=z7[:, lo:hi, :])
+
+        def new_m(i):
+            act(TANH, z5[:, i, :], z5[:, i, :])
+            nc.sync.dma_start(out=new_m_dram[:, i, :], in_=z5[:, i, :])
+
+        new_c(0)
+        new_c(1)
+        for i in range(T):
+            act(TANH, z5[:, i, :], flip_add(i, (z4, z6))[:])
+            nc.vector.tensor_tensor(out=z5[:, i, :], in0=z5[:, i, :], in1=z7[:, i, :], op=MULT)
+            if i in (1, 3):
+                new_c(i // 2 + 2)
+            if i >= LAG:
+                new_m(i - LAG)
+        for i in range(T - LAG, T):
+            new_m(i)

@@ -26,7 +26,7 @@ FLOPS = 2 * 2 * B * K * 8 * H
 CHUNKS = [(a, g) for g in (6, 7, 4, 5, 0, 1) for a in ("x", "m")] + [("x", 3), ("x", 2), ("m", 2), ("m", 3)]
 RAW_BUFS = 8
 PAIRS = [(i, i + 2) for i in range(0, T, 2)]
-LAG = 2
+LAG = 6
 
 
 def tile_nascell_kernel(tc, x, m_prev, c_prev, w_m, w_inputs, out_0, out_1):
@@ -255,11 +255,11 @@ def tile_nascell_kernel(tc, x, m_prev, c_prev, w_m, w_inputs, out_0, out_1):
 
         new_c(0)
         new_c(1)
+        new_c(2)
+        new_c(3)
         for i in range(T):
             act(TANH, z5[:, i, :], flip_add(i, (z4, z6))[:])
             nc.vector.tensor_tensor(out=z5[:, i, :], in0=z5[:, i, :], in1=z7[:, i, :], op=MULT)
-            if i in (1, 3):
-                new_c(i // 2 + 2)
             if i >= LAG:
                 new_m(i - LAG)
         for i in range(T - LAG, T):

@@ -76,7 +76,7 @@ def tile_nascell_kernel(tc, x, m_prev, c_prev, w_m, w_inputs, out_0, out_1):
             raw_tiles[n] = raw
 
         def load_act(s, j):
-            nc.sync.dma_start(out=a_raw[:, s, 2 * j:2 * j + 2, :], in_=act_dram[sides[s]][:, 2 * j:2 * j + 2, :])
+            nc.sync.dma_start(out=a_raw[:, s, 4 * j:4 * j + 4, :], in_=act_dram[sides[s]][:, 4 * j:4 * j + 4, :])
 
         def regroup(n):
             grouped = grpp.tile([P, H, PACK], BF16, tag="grouped", name="grouped", align_bytes=64)
@@ -180,7 +180,7 @@ def tile_nascell_kernel(tc, x, m_prev, c_prev, w_m, w_inputs, out_0, out_1):
 
         load_chunk(0)
         load_chunk(1)
-        for j in range(4):
+        for j in range(2):
             load_act(0, j)
             load_act(1, j)
         for n in range(2, RAW_BUFS):

@@ -119,6 +119,10 @@ def tile_nascell_kernel(tc, x, m_prev, c_prev, w_m, w_inputs, out_0, out_1):
             nc.scalar.copy(out=a_grp[:, s].bitcast(F32)[:, 2 * j:2 * j + 2, :, :],
                            in_=bank[:].rearrange("p (t u b) -> p t b u", t=2, u=2))
 
+        def copy_act_v(s, j, bank):
+            nc.vector.tensor_copy(out=a_grp[:, s].bitcast(F32)[:, 2 * j:2 * j + 2, :, :],
+                                  in_=bank[:].rearrange("p (t u b) -> p t b u", t=2, u=2))
+
         def quantise_act(s, j):
             cols = slice(2 * j * P, (2 * j + 2) * P)
             nc.vector.quantize_mx(
@@ -170,8 +174,8 @@ def tile_nascell_kernel(tc, x, m_prev, c_prev, w_m, w_inputs, out_0, out_1):
         def act(func, dst, src):
             nc.scalar.activation(out=dst, in_=src, func=func)
 
-        def gate_cols(g, func, dst):
-            for j in range(T):
+        def gate_cols(g, func, dst, which=range(T)):
+            for j in which:
                 act(func, dst[:, j, :], mx_cols(g, j)[:])
 
         def zt(name):
@@ -180,25 +184,49 @@ def tile_nascell_kernel(tc, x, m_prev, c_prev, w_m, w_inputs, out_0, out_1):
 
         load_chunk(0)
         load_chunk(1)
-        for j in range(2):
-            load_act(0, j)
-            load_act(1, j)
+        load_act(0, 0)
+        load_act(1, 0)
+        load_act(0, 1)
+        load_act(1, 1)
         for n in range(2, RAW_BUFS):
             load_chunk(n)
 
-        prepare(0, 2)
-        for j in range(4):
-            bx = transpose_act(0, j)
-            bm = transpose_act(1, j)
-            copy_act(0, j, bx)
-            copy_act(1, j, bm)
-            quantise_act(0, j)
-            quantise_act(1, j)
         z6 = zt("z6")
         z7 = zt("z7")
         z4 = zt("z4")
         z5 = zt("z5")
-        prepare(2, 2)
+        regroup(0)
+        regroup(1)
+        quantise(0)
+        quantise(1)
+        b00 = transpose_act(0, 0)
+        copy_act(0, 0, b00)
+        b01 = transpose_act(0, 1)
+        copy_act(0, 1, b01)
+        quantise_act(0, 0)
+        quantise_act(0, 1)
+        b10 = transpose_act(1, 0)
+        copy_act(1, 0, b10)
+        b11 = transpose_act(1, 1)
+        copy_act(1, 1, b11)
+        quantise_act(1, 0)
+        quantise_act(1, 1)
+        b02 = transpose_act(0, 2)
+        copy_act(0, 2, b02)
+        b03 = transpose_act(0, 3)
+        copy_act(0, 3, b03)
+        quantise_act(0, 2)
+        quantise_act(0, 3)
+        b12 = transpose_act(1, 2)
+        copy_act(1, 2, b12)
+        b13 = transpose_act(1, 3)
+        copy_act(1, 3, b13)
+        regroup(2)
+        quantise_act(1, 2)
+        quantise_act(1, 3)
+        regroup(3)
+        quantise(2)
+        quantise(3)
         gate_cols(6, TANH, z6)
         prepare(4, 2)
         gate_cols(7, SIGMOID, z7)

@@ -27,6 +27,7 @@ CHUNKS = [(a, g) for g in (6, 7, 4, 5, 0, 1) for a in ("x", "m")] + [("x", 3), (
 RAW_BUFS = 8
 PAIRS = [(i, i + 2) for i in range(0, T, 2)]
 LAG = 6
+PAD = 48
 
 
 def tile_nascell_kernel(tc, x, m_prev, c_prev, w_m, w_inputs, out_0, out_1):
@@ -55,13 +56,14 @@ def tile_nascell_kernel(tc, x, m_prev, c_prev, w_m, w_inputs, out_0, out_1):
         a_codes = {}
         a_scales = {}
         for a in sides:
-            a_codes[a] = keep.tile([P, T * P], U32, name="a_codes_%s" % a, align_bytes=64)
-            a_scales[a] = keep.tile([P, T * P], U8, name="a_scales_%s" % a, align_bytes=64)
+            a_codes[a] = keep.tile([P, T * P], U32, name="a_codes_%s" % a, align_bytes=256)
+            a_scales[a] = keep.tile([P, T * P], U8, name="a_scales_%s" % a, align_bytes=256)
         w_codes = {}
         w_scales = {}
         for a, g in CHUNKS:
-            w_codes[(a, g)] = keep.tile([P, H], U32, name="w_codes_%s%d" % (a, g), align_bytes=64)
-            w_scales[(a, g)] = keep.tile([P, H], U8, name="w_scales_%s%d" % (a, g), align_bytes=64)
+            padded = keep.tile([P, PAD + H], U32, name="w_codes_%s%d" % (a, g), align_bytes=256)
+            w_codes[(a, g)] = padded[:, PAD:PAD + H]
+            w_scales[(a, g)] = keep.tile([P, H], U8, name="w_scales_%s%d" % (a, g), align_bytes=256)
         c_sb = keep.tile([P, T, H], BF16)
         new_m_dram = out_0.rearrange("(p t) h -> p t h", t=T)
         new_c_dram = out_1.rearrange("(p t) h -> p t h", t=T)

@@ -26,6 +26,7 @@ FLOPS = 2 * 2 * B * K * 8 * H
 CHUNKS = [(a, g) for g in (6, 7, 4, 5, 0, 1) for a in ("x", "m")] + [("x", 3), ("x", 2), ("m", 2), ("m", 3)]
 RAW_BUFS = 8
 PAIRS = [(i, i + 2) for i in range(0, T, 2)]
+HALVES = [(0, 4), (4, 8)]
 LAG = 6
 PAD = 48
 
@@ -241,29 +242,29 @@ def tile_nascell_kernel(tc, x, m_prev, c_prev, w_m, w_inputs, out_0, out_1):
         gate_cols(0, SIGMOID, z0)
         for lo, hi in PAIRS:
             nc.vector.tensor_tensor(out=z4[:, lo:hi, :], in0=z4[:, lo:hi, :], in1=z5[:, lo:hi, :], op=MULT)
-        for n, (lo, hi) in enumerate(PAIRS):
-            back = PAIRS[len(PAIRS) - 1 - n]
-            nc.gpsimd.tensor_tensor(out=z5[:, back[0]:back[1], :], in0=z6[:, lo:hi, :], in1=z7[:, lo:hi, :], op=ADD)
+        for lo in (2, 0, 6, 4):
+            to = (lo + 4) % T
+            nc.gpsimd.tensor_tensor(out=z5[:, to:to + 2, :], in0=z6[:, lo:lo + 2, :], in1=z7[:, lo:lo + 2, :], op=ADD)
         for j in range(T):
             nc.vector.scalar_tensor_tensor(out=z0[:, j, :], in0=mx_cols(1, j)[:], scalar=0.0, in1=z0[:, j, :], op0=MAX, op1=MULT)
-        for lo, hi in PAIRS:
+        for lo, hi in HALVES:
             act(TANH, z4[:, lo:hi, :], z4[:, lo:hi, :])
         zx = zt("zx")
         for i in range(T):
             nc.vector.tensor_copy(out=zx[:, i, :], in_=mx_rows(3, i, ("x",))[:])
         sums = []
         for half in range(2):
-            for lo, hi in PAIRS[2 * half:2 * half + 2]:
-                act(TANH, z0[:, lo:hi, :], z0[:, lo:hi, :])
+            lo, hi = HALVES[half]
+            act(TANH, z0[:, lo:hi, :], z0[:, lo:hi, :])
             for i in range(Q * half, Q * half + Q):
                 sums.append(flip_add(i, (z0,), c_sb[:, i, :]))
         prepare(13, 2)
         prepare(15, 1)
         for i in range(T):
             act(TANH, z7[:, i, :], sums[i][:])
-        for n, (lo, hi) in enumerate(PAIRS):
-            back = PAIRS[len(PAIRS) - 1 - n]
-            act(SIGMOID, z6[:, lo:hi, :], z5[:, back[0]:back[1], :])
+        for half in range(2):
+            (lo, hi), (back, end) = HALVES[half], HALVES[1 - half]
+            act(SIGMOID, z6[:, lo:hi, :], z5[:, back:end, :])
         g2 = [mx_rows(2, i, sides) for i in range(Q)]
         for i in range(T):
             nc.vector.tensor_tensor(out=zx[:, i, :], in0=zx[:, i, :], in1=mx_rows(3, i, ("m",))[:], op=MULT)

@@ -23,7 +23,7 @@ T = B // P
 Q = H // P
 FLOPS = 2 * 2 * B * K * 8 * H
 
-CHUNKS = [(a, g) for g in (6, 7, 4, 5, 0, 1) for a in ("x", "m")] + [("x", 3), ("x", 2), ("m", 2), ("m", 3)]
+CHUNKS = [(a, g) for g in (6, 7, 4, 5, 0, 1) for a in ("x", "m")] + [("x", 3), ("m", 3), ("x", 2), ("m", 2)]
 RAW_BUFS = 8
 PAIRS = [(i, i + 2) for i in range(0, T, 2)]
 HALVES = [(0, 4), (4, 8)]
@@ -258,17 +258,16 @@ def tile_nascell_kernel(tc, x, m_prev, c_prev, w_m, w_inputs, out_0, out_1):
             act(TANH, z0[:, lo:hi, :], z0[:, lo:hi, :])
             for i in range(Q * half, Q * half + Q):
                 sums.append(flip_add(i, (z0,), c_sb[:, i, :]))
-        prepare(13, 2)
-        prepare(15, 1)
+        prepare(13, 1)
+        prepare(14, 2)
         for i in range(T):
             act(TANH, z7[:, i, :], sums[i][:])
         for half in range(2):
             (lo, hi), (back, end) = HALVES[half], HALVES[1 - half]
             act(SIGMOID, z6[:, lo:hi, :], z5[:, back:end, :])
-        g2 = [mx_rows(2, i, sides) for i in range(Q)]
         for i in range(T):
             nc.vector.tensor_tensor(out=zx[:, i, :], in0=zx[:, i, :], in1=mx_rows(3, i, ("m",))[:], op=MULT)
-        g2 += [mx_rows(2, i, sides) for i in range(Q, T)]
+        g2 = [mx_rows(2, i, sides) for i in range(T)]
         for i in range(T):
             act(SIGMOID, z0[:, i, :], g2[i][:])
         for lo, hi in PAIRS:

@@ -28,6 +28,7 @@ RAW_BUFS = 8
 PAIRS = [(i, i + 2) for i in range(0, T, 2)]
 HALVES = [(0, 4), (4, 8)]
 LAG = 6
+AHEAD = 6
 PAD = 48
 
 
@@ -37,7 +38,7 @@ def tile_nascell_kernel(tc, x, m_prev, c_prev, w_m, w_inputs, out_0, out_1):
         keep = ctx.enter_context(tc.tile_pool(name="keep", bufs=1))
         rawp = ctx.enter_context(tc.tile_pool(name="rawp", bufs=RAW_BUFS))
         grpp = ctx.enter_context(tc.tile_pool(name="grpp", bufs=4))
-        big = ctx.enter_context(tc.tile_pool(name="big", bufs=6))
+        big = ctx.enter_context(tc.tile_pool(name="big", bufs=7))
         psum = ctx.enter_context(tc.psum_pool(name="psum", bufs=8))
         ctx.enter_context(tc.manual_schedule())
 
@@ -240,11 +241,11 @@ def tile_nascell_kernel(tc, x, m_prev, c_prev, w_m, w_inputs, out_0, out_1):
         prepare(10, 3)
         z0 = zt("z0")
         gate_cols(0, SIGMOID, z0)
-        for lo, hi in PAIRS:
+        for lo, hi in HALVES:
             nc.vector.tensor_tensor(out=z4[:, lo:hi, :], in0=z4[:, lo:hi, :], in1=z5[:, lo:hi, :], op=MULT)
-        for lo in (2, 0, 6, 4):
-            to = (lo + 4) % T
-            nc.gpsimd.tensor_tensor(out=z5[:, to:to + 2, :], in0=z6[:, lo:lo + 2, :], in1=z7[:, lo:lo + 2, :], op=ADD)
+        for half in range(2):
+            (lo, hi), (to, end) = HALVES[half], HALVES[1 - half]
+            nc.gpsimd.tensor_tensor(out=z5[:, to:end, :], in0=z6[:, lo:hi, :], in1=z7[:, lo:hi, :], op=ADD)
         for j in range(T):
             nc.vector.scalar_tensor_tensor(out=z0[:, j, :], in0=mx_cols(1, j)[:], scalar=0.0, in1=z0[:, j, :], op0=MAX, op1=MULT)
         for lo, hi in HALVES:
@@ -260,14 +261,18 @@ def tile_nascell_kernel(tc, x, m_prev, c_prev, w_m, w_inputs, out_0, out_1):
                 sums.append(flip_add(i, (z0,), c_sb[:, i, :]))
         prepare(13, 1)
         prepare(14, 2)
+        z8 = zt("z8")
         for i in range(T):
-            act(TANH, z7[:, i, :], sums[i][:])
+            act(TANH, z8[:, i, :], sums[i][:])
         for half in range(2):
             (lo, hi), (back, end) = HALVES[half], HALVES[1 - half]
             act(SIGMOID, z6[:, lo:hi, :], z5[:, back:end, :])
+        g2 = []
         for i in range(T):
+            if i >= AHEAD:
+                g2.append(mx_rows(2, i - AHEAD, sides))
             nc.vector.tensor_tensor(out=zx[:, i, :], in0=zx[:, i, :], in1=mx_rows(3, i, ("m",))[:], op=MULT)
-        g2 = [mx_rows(2, i, sides) for i in range(T)]
+        g2 += [mx_rows(2, i, sides) for i in range(T - AHEAD, T)]
         for i in range(T):
             act(SIGMOID, z0[:, i, :], g2[i][:])
         for lo, hi in PAIRS:
@@ -276,8 +281,8 @@ def tile_nascell_kernel(tc, x, m_prev, c_prev, w_m, w_inputs, out_0, out_1):
             act(TANH, zx[:, lo:hi, :], zx[:, lo:hi, :])
         def new_c(n):
             lo, hi = PAIRS[n]
-            nc.vector.tensor_tensor(out=z7[:, lo:hi, :], in0=z7[:, lo:hi, :], in1=zx[:, lo:hi, :], op=MULT)
-            nc.sync.dma_start(out=new_c_dram[:, lo:hi, :], in_=z7[:, lo:hi, :])
+            nc.vector.tensor_tensor(out=z8[:, lo:hi, :], in0=z8[:, lo:hi, :], in1=zx[:, lo:hi, :], op=MULT)
+            nc.sync.dma_start(out=new_c_dram[:, lo:hi, :], in_=z8[:, lo:hi, :])
 
         def new_m(i):
             act(TANH, z5[:, i, :], z5[:, i, :])
@@ -289,7 +294,7 @@ def tile_nascell_kernel(tc, x, m_prev, c_prev, w_m, w_inputs, out_0, out_1):
         new_c(3)
         for i in range(T):
             act(TANH, z5[:, i, :], flip_add(i, (z4, z6))[:])
-            nc.vector.tensor_tensor(out=z5[:, i, :], in0=z5[:, i, :], in1=z7[:, i, :], op=MULT)
+            nc.vector.tensor_tensor(out=z5[:, i, :], in0=z5[:, i, :], in1=z8[:, i, :], op=MULT)
             if i >= LAG:
                 new_m(i - LAG)
         for i in range(T - LAG, T):

@@ -27,8 +27,8 @@ CHUNKS = [(a, g) for g in (6, 7, 4, 5, 0, 1) for a in ("x", "m")] + [("x", 3), (
 RAW_BUFS = 8
 PAIRS = [(i, i + 2) for i in range(0, T, 2)]
 HALVES = [(0, 4), (4, 8)]
-LAG = 6
-AHEAD = 6
+LAG = 5
+AHEAD = 5
 PAD = 48
 
 
@@ -187,8 +187,8 @@ def tile_nascell_kernel(tc, x, m_prev, c_prev, w_m, w_inputs, out_0, out_1):
             return z
 
         load_chunk(0)
-        load_chunk(1)
         load_act(0, 0)
+        load_chunk(1)
         load_act(1, 0)
         load_act(0, 1)
         load_act(1, 1)
@@ -200,15 +200,15 @@ def tile_nascell_kernel(tc, x, m_prev, c_prev, w_m, w_inputs, out_0, out_1):
         z4 = zt("z4")
         z5 = zt("z5")
         regroup(0)
-        regroup(1)
         quantise(0)
-        quantise(1)
         b00 = transpose_act(0, 0)
         copy_act(0, 0, b00)
         b01 = transpose_act(0, 1)
         copy_act(0, 1, b01)
         quantise_act(0, 0)
         quantise_act(0, 1)
+        regroup(1)
+        quantise(1)
         b10 = transpose_act(1, 0)
         copy_act(1, 0, b10)
         b11 = transpose_act(1, 1)
@@ -291,10 +291,11 @@ def tile_nascell_kernel(tc, x, m_prev, c_prev, w_m, w_inputs, out_0, out_1):
         new_c(0)
         new_c(1)
         new_c(2)
-        new_c(3)
         for i in range(T):
             act(TANH, z5[:, i, :], flip_add(i, (z4, z6))[:])
             nc.vector.tensor_tensor(out=z5[:, i, :], in0=z5[:, i, :], in1=z8[:, i, :], op=MULT)
+            if i == 0:
+                new_c(3)
             if i >= LAG:
                 new_m(i - LAG)
         for i in range(T - LAG, T):

from contextlib import ExitStack

import concourse.mybir as mybir
from concourse.masks import make_identity

F32 = mybir.dt.float32
BF16 = mybir.dt.bfloat16
U32 = mybir.dt.uint32
U8 = mybir.dt.uint8
FP8X4 = mybir.dt.float8_e4m3fn_x4
TANH = mybir.ActivationFunctionType.Tanh
SIGMOID = mybir.ActivationFunctionType.Sigmoid
ADD = mybir.AluOpType.add
MULT = mybir.AluOpType.mult
MAX = mybir.AluOpType.max

P = 128
PACK = 4
B = 1024
K = 512
H = 512
T = B // P
Q = H // P
FLOPS = 2 * 2 * B * K * 8 * H

CHUNKS = [(a, g) for g in (6, 7, 4, 5, 0, 1) for a in ("x", "m")] + [("x", 3), ("m", 3), ("x", 2), ("m", 2)]
RAW_BUFS = 8
PAIRS = [(i, i + 2) for i in range(0, T, 2)]
HALVES = [(0, 4), (4, 8)]
LAG = 5
AHEAD = 5
PAD = 48


def tile_nascell_kernel(tc, x, m_prev, c_prev, w_m, w_inputs, out_0, out_1):
    nc = tc.nc
    with ExitStack() as ctx:
        keep = ctx.enter_context(tc.tile_pool(name="keep", bufs=1))
        rawp = ctx.enter_context(tc.tile_pool(name="rawp", bufs=RAW_BUFS))
        grpp = ctx.enter_context(tc.tile_pool(name="grpp", bufs=4))
        big = ctx.enter_context(tc.tile_pool(name="big", bufs=7))
        psum = ctx.enter_context(tc.psum_pool(name="psum", bufs=8))
        ctx.enter_context(tc.manual_schedule())

        warm = keep.tile([P, 1], F32)
        nc.vector.memset(warm[:], 0.0)
        nc.scalar.activation(out=warm[:], in_=warm[:], func=SIGMOID)
        ident = keep.tile([P, P], F32)
        make_identity(nc, ident[:])
        ident_bf = keep.tile([P, P], BF16)
        make_identity(nc, ident_bf[:])

        sides = ("x", "m")
        act_dram = {"x": x.rearrange("(p t) k -> p t k", t=T), "m": m_prev.rearrange("(p t) k -> p t k", t=T)}
        w_dram = {"x": w_inputs, "m": w_m}
        a_raw = big.tile([P, 2, T, K], BF16, tag="big", name="a_raw", align_bytes=64)
        a_grp = big.tile([P, 2, T, P, PACK], BF16, tag="big", name="a_grp", align_bytes=64)
        a_codes = {}
        a_scales = {}
        for a in sides:
            a_codes[a] = keep.tile([P, T * P], U32, name="a_codes_%s" % a, align_bytes=256)
            a_scales[a] = keep.tile([P, T * P], U8, name="a_scales_%s" % a, align_bytes=256)
        w_codes = {}
        w_scales = {}
        for a, g in CHUNKS:
            padded = keep.tile([P, PAD + H], U32, name="w_codes_%s%d" % (a, g), align_bytes=256)
            w_codes[(a, g)] = padded[:, PAD:PAD + H]
            w_scales[(a, g)] = keep.tile([P, H], U8, name="w_scales_%s%d" % (a, g), align_bytes=256)
        c_sb = keep.tile([P, T, H], BF16)
        new_m_dram = out_0.rearrange("(p t) h -> p t h", t=T)
        new_c_dram = out_1.rearrange("(p t) h -> p t h", t=T)

        raw_tiles = {}
        grp_tiles = {}

        def load_chunk(n):
            a, g = CHUNKS[n]
            raw = rawp.tile([P, PACK, H], BF16)
            nc.sync.dma_start(out=raw[:], in_=w_dram[a][:, g * H:(g + 1) * H].rearrange("(p j) c -> p j c", j=PACK))
            raw_tiles[n] = raw

        def load_act(s, j):
            nc.sync.dma_start(out=a_raw[:, s, 4 * j:4 * j + 4, :], in_=act_dram[sides[s]][:, 4 * j:4 * j + 4, :])

        def regroup(n):
            grouped = grpp.tile([P, H, PACK], BF16, tag="grouped", name="grouped", align_bytes=64)
            nc.vector.tensor_copy(
                out=grouped[:].rearrange("p (c i) t -> p c t i", i=4),
                in_=raw_tiles[n][:].rearrange("p t (c i) -> p c t i", i=4),
            )
            grp_tiles[n] = grouped
            if n + RAW_BUFS < len(CHUNKS):
                load_chunk(n + RAW_BUFS)
            if n + RAW_BUFS == len(CHUNKS) - 5:
                nc.sync.dma_start(out=c_sb[:], in_=c_prev.rearrange("(p t) h -> p t h", t=T))

        def quantise(n):
            nc.vector.quantize_mx(
                out=w_codes[CHUNKS[n]][:].bitcast(FP8X4),
                scales=w_scales[CHUNKS[n]][:],
                in_=grp_tiles[n][:].rearrange("p c t -> p (c t)"),
            )

        def prepare(first, count):
            for n in range(first, first + count):
                regroup(n)
            for n in range(first, first + count):
                quantise(n)

        def new_bank():
            bank = psum.tile([P, H], F32, tag="bank", name="bank")
            return bank

        def transpose_act(s, j):
            words = a_raw[:, s].bitcast(F32).rearrange("p t (q u) -> p t u q", u=2)
            bank = new_bank()
            for tt in range(2):
                for u in range(2):
                    nc.tensor.transpose(bank[:, (2 * tt + u) * P:(2 * tt + u + 1) * P], words[:, 2 * j + tt, u, :], ident[:])
            return bank

        def copy_act(s, j, bank):
            nc.scalar.copy(out=a_grp[:, s].bitcast(F32)[:, 2 * j:2 * j + 2, :, :],
                           in_=bank[:].rearrange("p (t u b) -> p t b u", t=2, u=2))

        def copy_act_v(s, j, bank):
            nc.vector.tensor_copy(out=a_grp[:, s].bitcast(F32)[:, 2 * j:2 * j + 2, :, :],
                                  in_=bank[:].rearrange("p (t u b) -> p t b u", t=2, u=2))

        def quantise_act(s, j):
            cols = slice(2 * j * P, (2 * j + 2) * P)
            nc.vector.quantize_mx(
                out=a_codes[sides[s]][:, cols].bitcast(FP8X4),
                scales=a_scales[sides[s]][:, cols],
                in_=a_grp[:, s, 2 * j:2 * j + 2].rearrange("p t b k -> p (t b k)"),
            )

        def mx_rows(g, i, which):
            bank = new_bank()
            rows = slice(i * P, (i + 1) * P)
            for s, a in enumerate(which):
                nc.tensor.matmul_mx(
                    out=bank[:],
                    lhsT=a_codes[a][:, rows].bitcast(FP8X4), lhsT_scale=a_scales[a][:, rows],
                    rhs=w_codes[(a, g)][:].bitcast(FP8X4), rhs_scale=w_scales[(a, g)][:],
                    start=(s == 0), stop=(s == len(which) - 1),
                )
            return bank

        def mx_cols(g, j):
            bank = new_bank()
            cols = slice((j % Q) * P, (j % Q + 1) * P)
            half = slice((j // Q) * H, (j // Q + 1) * H)
            for s, a in enumerate(sides):
                nc.tensor.matmul_mx(
                    out=bank[:],
                    lhsT=w_codes[(a, g)][:, cols].bitcast(FP8X4), lhsT_scale=w_scales[(a, g)][:, cols],
                    rhs=a_codes[a][:, half].bitcast(FP8X4), rhs_scale=a_scales[a][:, half],
                    start=(s == 0), stop=(s == 1),
                )
            return bank

        def block(z, q, i):
            return z[:, Q * (i // Q) + q, (i % Q) * P:(i % Q + 1) * P]

        def flip_add(i, terms, plain=None):
            bank = new_bank()
            if plain is not None:
                nc.tensor.matmul(out=bank[:], lhsT=ident_bf[:], rhs=plain, start=True, stop=False)
            count = 0
            for z in terms:
                for q in range(Q):
                    count += 1
                    nc.tensor.matmul(out=bank[:, q * P:(q + 1) * P], lhsT=block(z, q, i), rhs=ident[:], is_transpose=True,
                                     start=(plain is None and count == 1), stop=(count == Q * len(terms)))
            return bank

        def act(func, dst, src):
            nc.scalar.activation(out=dst, in_=src, func=func)

        def gate_cols(g, func, dst, which=range(T)):
            for j in which:
                act(func, dst[:, j, :], mx_cols(g, j)[:])

        def zt(name):
            z = big.tile([P, T, H], F32, tag="big", name=name, align_bytes=64)
            return z

        load_chunk(0)
        load_act(0, 0)
        load_chunk(1)
        load_act(1, 0)
        load_act(0, 1)
        load_act(1, 1)
        for n in range(2, RAW_BUFS):
            load_chunk(n)

        z6 = zt("z6")
        z7 = zt("z7")
        z4 = zt("z4")
        z5 = zt("z5")
        regroup(0)
        quantise(0)
        b00 = transpose_act(0, 0)
        copy_act(0, 0, b00)
        b01 = transpose_act(0, 1)
        copy_act(0, 1, b01)
        quantise_act(0, 0)
        quantise_act(0, 1)
        regroup(1)
        quantise(1)
        b10 = transpose_act(1, 0)
        copy_act(1, 0, b10)
        b11 = transpose_act(1, 1)
        copy_act(1, 1, b11)
        quantise_act(1, 0)
        quantise_act(1, 1)
        b02 = transpose_act(0, 2)
        copy_act(0, 2, b02)
        b03 = transpose_act(0, 3)
        copy_act(0, 3, b03)
        quantise_act(0, 2)
        quantise_act(0, 3)
        b12 = transpose_act(1, 2)
        copy_act(1, 2, b12)
        b13 = transpose_act(1, 3)
        copy_act(1, 3, b13)
        regroup(2)
        quantise_act(1, 2)
        quantise_act(1, 3)
        regroup(3)
        quantise(2)
        quantise(3)
        gate_cols(6, TANH, z6)
        prepare(4, 2)
        gate_cols(7, SIGMOID, z7)
        prepare(6, 2)
        gate_cols(4, TANH, z4)
        prepare(8, 2)
        gate_cols(5, SIGMOID, z5)
        prepare(10, 3)
        z0 = zt("z0")
        gate_cols(0, SIGMOID, z0)
        for lo, hi in HALVES:
            nc.vector.tensor_tensor(out=z4[:, lo:hi, :], in0=z4[:, lo:hi, :], in1=z5[:, lo:hi, :], op=MULT)
        for half in range(2):
            (lo, hi), (to, end) = HALVES[half], HALVES[1 - half]
            nc.gpsimd.tensor_tensor(out=z5[:, to:end, :], in0=z6[:, lo:hi, :], in1=z7[:, lo:hi, :], op=ADD)
        for j in range(T):
            nc.vector.scalar_tensor_tensor(out=z0[:, j, :], in0=mx_cols(1, j)[:], scalar=0.0, in1=z0[:, j, :], op0=MAX, op1=MULT)
        for lo, hi in HALVES:
            act(TANH, z4[:, lo:hi, :], z4[:, lo:hi, :])
        zx = zt("zx")
        for i in range(T):
            nc.vector.tensor_copy(out=zx[:, i, :], in_=mx_rows(3, i, ("x",))[:])
        sums = []
        for half in range(2):
            lo, hi = HALVES[half]
            act(TANH, z0[:, lo:hi, :], z0[:, lo:hi, :])
            for i in range(Q * half, Q * half + Q):
                sums.append(flip_add(i, (z0,), c_sb[:, i, :]))
        prepare(13, 1)
        prepare(14, 2)
        z8 = zt("z8")
        for i in range(T):
            act(TANH, z8[:, i, :], sums[i][:])
        for half in range(2):
            (lo, hi), (back, end) = HALVES[half], HALVES[1 - half]
            act(SIGMOID, z6[:, lo:hi, :], z5[:, back:end, :])
        g2 = []
        for i in range(T):
            if i >= AHEAD:
                g2.append(mx_rows(2, i - AHEAD, sides))
            nc.vector.tensor_tensor(out=zx[:, i, :], in0=zx[:, i, :], in1=mx_rows(3, i, ("m",))[:], op=MULT)
        g2 += [mx_rows(2, i, sides) for i in range(T - AHEAD, T)]
        for i in range(T):
            act(SIGMOID, z0[:, i, :], g2[i][:])
        for lo, hi in PAIRS:
            nc.vector.scalar_tensor_tensor(out=zx[:, lo:hi, :], in0=zx[:, lo:hi, :], scalar=0.0, in1=z0[:, lo:hi, :], op0=MAX, op1=ADD)
        for lo, hi in PAIRS:
            act(TANH, zx[:, lo:hi, :], zx[:, lo:hi, :])
        def new_c(n):
            lo, hi = PAIRS[n]
            nc.vector.tensor_tensor(out=z8[:, lo:hi, :], in0=z8[:, lo:hi, :], in1=zx[:, lo:hi, :], op=MULT)
            nc.sync.dma_start(out=new_c_dram[:, lo:hi, :], in_=z8[:, lo:hi, :])

        def new_m(i):
            act(TANH, z5[:, i, :], z5[:, i, :])
            nc.sync.dma_start(out=new_m_dram[:, i, :], in_=z5[:, i, :])

        new_c(0)
        new_c(1)
        new_c(2)
        for i in range(T):
            act(TANH, z5[:, i, :], flip_add(i, (z4, z6))[:])
            nc.vector.tensor_tensor(out=z5[:, i, :], in0=z5[:, i, :], in1=z8[:, i, :], op=MULT)
            if i == 0:
                new_c(3)
            if i >= LAG:
                new_m(i - LAG)
        for i in range(T - LAG, T):
            new_m(i)
